import numpy as np
import ml_dtypes


def mxq(x, axis, fmt="e4m3"):
    dtype, down = {"e4m3": (ml_dtypes.float8_e4m3fn, 7), "e5m2": (ml_dtypes.float8_e5m2, 14)}[fmt]
    v = np.moveaxis(np.asarray(x, np.float32).astype(ml_dtypes.bfloat16).astype(np.float64), axis, -1)
    blocks = v.reshape(v.shape[:-1] + (-1, 32))
    amax = np.abs(blocks).max(-1, keepdims=True)
    byte = np.maximum(np.where(amax > 0, np.frexp(amax)[1] - 1 + 127, 0) - down, 1)
    scale = np.exp2(byte - 127.0)
    codes = (blocks / scale).astype(np.float32).astype(dtype).astype(np.float64)
    return np.moveaxis((codes * scale).reshape(v.shape), -1, axis)


WIDE = False


def mx_kscale(k):
    if not WIDE:
        return np.ones(k)
    levels = np.array([10, -10, 5, -5, 0])
    a = np.random.permutation(np.resize(levels, k // 512 * 4)).reshape(k // 512, 4)
    idx = np.arange(k)
    return np.exp2(a[idx // 512, idx % 128 // 32])


BF16 = ml_dtypes.bfloat16


def bf(x):
    return np.asarray(x, np.float32).astype(BF16)


def f64(x):
    return np.asarray(x).astype(np.float64)


B, CIN, P, COUT, W, H, HEADS = 2, 1024, 512, 2048, 16, 32, 4
N = W * H
EPS = 1e-5


def bn(y, g, b, m, v):
    return (y - f64(m)[None, :, None]) * (f64(g) / np.sqrt(f64(v) + EPS))[None, :, None] + f64(b)[None, :, None]


def setup_inputs():
    s, t = mx_kscale(P), mx_kscale(CIN)
    return {
        "h_attn": bf(np.maximum(np.random.standard_normal((B, P, N)), 0.0) * s[None, :, None]),
        "x": bf(np.random.standard_normal((B, CIN, N)) * t[None, :, None]),
        "conv3_w": bf(np.random.standard_normal((COUT, P)) * 1.5 / np.sqrt(P) / s[None, :]),
        "bn3_g": bf(np.random.uniform(0.5, 1.5, COUT)),
        "bn3_b": bf(np.random.standard_normal(COUT) * 0.3),
        "bn3_m": bf(np.random.standard_normal(COUT) * 0.3),
        "bn3_v": bf(np.random.uniform(0.5, 1.5, COUT)),
        "sc_w": bf(np.random.standard_normal((COUT, CIN)) / np.sqrt(CIN) / t[None, :]),
        "sc_b": bf(np.random.standard_normal(COUT) * 0.3),
        "scbn_g": bf(np.random.uniform(0.5, 1.5, COUT)),
        "scbn_b": bf(np.random.standard_normal(COUT) * 0.3),
        "scbn_m": bf(np.random.standard_normal(COUT) * 0.3),
        "scbn_v": bf(np.random.uniform(0.5, 1.5, COUT)),
    }


def reference(h_attn, x, conv3_w, bn3_g, bn3_b, bn3_m, bn3_v, sc_w, sc_b, scbn_g, scbn_b, scbn_m, scbn_v):
    main = bn(mxq(f64(conv3_w), 1, "e4m3") @ mxq(f64(h_attn), 1, "e4m3"), bn3_g, bn3_b, bn3_m, bn3_v)
    short = (mxq(f64(sc_w), 1, "e4m3") @ mxq(f64(x), 1, "e4m3")) + f64(sc_b)[None, :, None]
    short = bn(short, scbn_g, scbn_b, scbn_m, scbn_v)
    return np.maximum(main + short, 0.0)

@@ -1,0 +1,172 @@
+from contextlib import ExitStack
+
+import concourse.mybir as mybir
+from concourse.masks import make_identity
+
+F32 = mybir.dt.float32
+BF16 = mybir.dt.bfloat16
+U32 = mybir.dt.uint32
+U8 = mybir.dt.uint8
+FP8X4 = mybir.dt.float8_e4m3fn_x4
+ACT = mybir.ActivationFunctionType
+ALU = mybir.AluOpType
+
+P = 128
+PACK = 4
+K_PASS = P * PACK
+BATCH = 2
+POSITIONS = 512
+C_MAIN = 512
+C_SHORT = 1024
+C_ALL = C_MAIN + C_SHORT
+PASSES = C_ALL // K_PASS
+C_OUT = 2048
+SLOTS = C_OUT // P
+GROUP = 2
+GROUPS = SLOTS // GROUP
+HALF = K_PASS // 2
+UNITS_PER_BANK = 2
+BANKS_PER_GROUP = GROUP * PASSES // UNITS_PER_BANK
+EPS = 1e-5
+
+FLOPS = 2 * BATCH * C_OUT * C_ALL * POSITIONS
+
+
+def tile_bottleneck_transformer_pb_kernel(
+    tc, h_attn, x, conv3_w, bn3_g, bn3_b, bn3_m, bn3_v, sc_w, sc_b, scbn_g, scbn_b, scbn_m, scbn_v, out
+):
+    nc = tc.nc
+    with ExitStack() as ctx:
+        keep = ctx.enter_context(tc.tile_pool(name="keep", bufs=1))
+        stage = ctx.enter_context(tc.tile_pool(name="stage", bufs=3))
+        results = ctx.enter_context(tc.tile_pool(name="results", bufs=6))
+        banks = ctx.enter_context(tc.psum_pool(name="banks", bufs=8))
+
+        w_raw = keep.tile([P, SLOTS * C_ALL], BF16)
+        w_raw_slots = w_raw[:].rearrange("p (c k) -> p c k", c=SLOTS)
+        conv3_slots = conv3_w.rearrange("(p c) k -> p c k", c=SLOTS)
+        sc_slots = sc_w.rearrange("(p c) k -> p c k", c=SLOTS)
+        act_raw = [keep.tile([P, 2 * PASSES, 2, POSITIONS], BF16, name="act_raw%d" % b) for b in range(BATCH)]
+
+        def load_weights(g):
+            slots = slice(g * GROUP, (g + 1) * GROUP)
+            nc.sync.dma_start(out=w_raw_slots[:, slots, 0:C_MAIN], in_=conv3_slots[:, slots, :])
+            nc.sync.dma_start(out=w_raw_slots[:, slots, C_MAIN:C_ALL], in_=sc_slots[:, slots, :])
+
+        def load_main_activations(b):
+            nc.sync.dma_start(out=act_raw[b][:, 0:2], in_=h_attn[b].rearrange("(s p e) n -> p s e n", p=P, e=2))
+
+        def load_short_activations(b):
+            nc.sync.dma_start(out=act_raw[b][:, 2:6], in_=x[b].rearrange("(s p e) n -> p s e n", p=P, e=2))
+
+        load_main_activations(0)
+        load_weights(0)
+        load_short_activations(0)
+        for g in range(1, GROUPS):
+            load_weights(g)
+        load_main_activations(1)
+        load_short_activations(1)
+
+        vectors = keep.tile([P, 9, SLOTS], BF16)
+        V_VAR, V_GAIN, V_MEAN, V_SHIFT, V_BIAS = 0, 2, 4, 6, 8
+        for i, vec in enumerate((bn3_v, scbn_v, bn3_g, scbn_g, bn3_m, scbn_m, bn3_b, scbn_b, sc_b)):
+            nc.scalar.dma_start(out=vectors[:, i, :], in_=vec.rearrange("(p c) -> p c", c=SLOTS))
+
+        identity = keep.tile([P, P], F32)
+        make_identity(nc, identity[:])
+
+        spread = keep.tile([P, 2, SLOTS], F32)
+        nc.vector.tensor_scalar_add(out=spread[:], in0=vectors[:, V_VAR : V_VAR + 2, :], scalar1=EPS)
+        nc.scalar.sqrt(out=spread[:], in_=spread[:])
+        gain = keep.tile([P, 2, SLOTS], F32)
+        nc.vector.reciprocal(out=gain[:], in_=spread[:])
+        nc.vector.tensor_mul(out=gain[:], in0=gain[:], in1=vectors[:, V_GAIN : V_GAIN + 2, :])
+        centre = keep.tile([P, 2, SLOTS], F32)
+        nc.vector.tensor_copy(out=centre[:, 0, :], in_=vectors[:, V_MEAN, :])
+        nc.vector.tensor_sub(out=centre[:, 1, :], in0=vectors[:, V_MEAN + 1, :], in1=vectors[:, V_BIAS, :])
+        nc.vector.tensor_mul(out=centre[:], in0=centre[:], in1=gain[:])
+        shift = keep.tile([P, SLOTS], F32)
+        nc.vector.tensor_add(out=shift[:], in0=vectors[:, V_SHIFT, :], in1=vectors[:, V_SHIFT + 1, :])
+        nc.vector.tensor_sub(out=shift[:], in0=shift[:], in1=centre[:, 0, :])
+        nc.vector.tensor_sub(out=shift[:], in0=shift[:], in1=centre[:, 1, :])
+
+        act_codes = [keep.tile([P, PASSES, POSITIONS], U32, name="act_codes%d" % b, align_bytes=64) for b in range(BATCH)]
+        act_scales = [keep.tile([P, PASSES, POSITIONS], U8, name="act_scales%d" % b, align_bytes=64) for b in range(BATCH)]
+        w_codes = keep.tile([P, SLOTS * PASSES * P], U32, align_bytes=64)
+        w_scales = keep.tile([P, SLOTS * PASSES * P], U8, align_bytes=64)
+
+        def quantise_activations(b, k_pass):
+            rows = act_raw[b][:, 2 * k_pass : 2 * k_pass + 2]
+            grouped = stage.tile([P, POSITIONS, PACK], BF16, name="act_grouped", align_bytes=64)
+            nc.vector.tensor_copy(
+                out=grouped[:].rearrange("p (c i) t -> p c t i", i=4),
+                in_=rows.rearrange("p s e (c i) -> p c (s e) i", i=4),
+            )
+            nc.vector.quantize_mx(
+                out=act_codes[b][:, k_pass, :].bitcast(FP8X4),
+                scales=act_scales[b][:, k_pass, :],
+                in_=grouped[:].rearrange("p n t -> p (n t)"),
+            )
+
+        w_words = w_raw[:].bitcast(F32)
+
+        def quantise_weights(g):
+            for j in range(g * BANKS_PER_GROUP, (g + 1) * BANKS_PER_GROUP):
+                turned = banks.tile([P, UNITS_PER_BANK, 2, P], F32, name="turned", tag="bank")
+                for a in range(UNITS_PER_BANK):
+                    for u in range(2):
+                        first = ((j * UNITS_PER_BANK + a) * 2 + u) * P
+                        nc.tensor.transpose(turned[:, a, u, :], w_words[:, first : first + P], identity[:])
+                grouped = stage.tile([P, UNITS_PER_BANK * P * PACK], BF16, name="w_grouped", align_bytes=64)
+                nc.scalar.copy(
+                    out=grouped[:].bitcast(F32).rearrange("p (a m u) -> p a m u", a=UNITS_PER_BANK, u=2),
+                    in_=turned[:].rearrange("p a u m -> p a m u"),
+                )
+                cols = slice(j * UNITS_PER_BANK * P, (j + 1) * UNITS_PER_BANK * P)
+                nc.vector.quantize_mx(out=w_codes[:, cols].bitcast(FP8X4), scales=w_scales[:, cols], in_=grouped[:])
+
+        def multiply(acc, b, c, passes):
+            for k_pass in passes:
+                cols = slice((c * PASSES + k_pass) * P, (c * PASSES + k_pass + 1) * P)
+                nc.tensor.matmul_mx(
+                    out=acc[:],
+                    lhsT=w_codes[:, cols].bitcast(FP8X4),
+                    lhsT_scale=w_scales[:, cols],
+                    rhs=act_codes[b][:, k_pass, :].bitcast(FP8X4),
+                    rhs_scale=act_scales[b][:, k_pass, :],
+                    start=(k_pass == passes[0]),
+                    stop=(k_pass == passes[-1]),
+                )
+
+        out_slots = [out[b].rearrange("(p c) n -> p c n", c=SLOTS) for b in range(BATCH)]
+
+        def finish_group(b, g):
+            result = results.tile([P, GROUP, POSITIONS], F32, name="result")
+            for i in range(GROUP):
+                c = g * GROUP + i
+                main = banks.tile([P, POSITIONS], F32, name="main", tag="bank")
+                multiply(main, b, c, (0,))
+                short = banks.tile([P, POSITIONS], F32, name="short", tag="bank")
+                multiply(short, b, c, (1, 2))
+                main_bn = stage.tile([P, POSITIONS], F32, name="main_bn")
+                nc.scalar.activation(
+                    out=main_bn[:], in_=main[:], func=ACT.Identity, scale=gain[:, 0, c : c + 1], bias=shift[:, c : c + 1]
+                )
+                nc.vector.scalar_tensor_tensor(
+                    out=result[:, i, :], in0=short[:], scalar=gain[:, 1, c : c + 1], in1=main_bn[:], op0=ALU.mult, op1=ALU.add
+                )
+            nc.vector.tensor_scalar_max(out=result[:], in0=result[:], scalar1=0.0)
+            nc.sync.dma_start(out=out_slots[b][:, g * GROUP : (g + 1) * GROUP, :], in_=result[:])
+
+        for k_pass in range(PASSES):
+            quantise_activations(0, k_pass)
+        quantise_weights(0)
+        for g in range(GROUPS):
+            if g + 1 < GROUPS:
+                quantise_weights(g + 1)
+            finish_group(0, g)
+            if g >= GROUPS - PASSES:
+                quantise_activations(1, g - (GROUPS - PASSES))
+
+        for g in range(GROUPS):
+            finish_group(1, g)

@@ -38,7 +38,7 @@ def tile_bottleneck_transformer_pb_kernel(
     nc = tc.nc
     with ExitStack() as ctx:
         keep = ctx.enter_context(tc.tile_pool(name="keep", bufs=1))
-        stage = ctx.enter_context(tc.tile_pool(name="stage", bufs=3))
+        stage = ctx.enter_context(tc.tile_pool(name="stage", bufs=4))
         results = ctx.enter_context(tc.tile_pool(name="results", bufs=6))
         banks = ctx.enter_context(tc.psum_pool(name="banks", bufs=8))
 
@@ -53,19 +53,20 @@ def tile_bottleneck_transformer_pb_kernel(
             nc.sync.dma_start(out=w_raw_slots[:, slots, 0:C_MAIN], in_=conv3_slots[:, slots, :])
             nc.sync.dma_start(out=w_raw_slots[:, slots, C_MAIN:C_ALL], in_=sc_slots[:, slots, :])
 
-        def load_main_activations(b):
-            nc.sync.dma_start(out=act_raw[b][:, 0:2], in_=h_attn[b].rearrange("(s p e) n -> p s e n", p=P, e=2))
+        def load_activations(b, k_pass):
+            rows = h_attn[b] if k_pass == 0 else x[b, (k_pass - 1) * K_PASS : k_pass * K_PASS, :]
+            nc.sync.dma_start(
+                out=act_raw[b][:, 2 * k_pass : 2 * k_pass + 2], in_=rows.rearrange("(s p e) n -> p s e n", p=P, e=2)
+            )
 
-        def load_short_activations(b):
-            nc.sync.dma_start(out=act_raw[b][:, 2:6], in_=x[b].rearrange("(s p e) n -> p s e n", p=P, e=2))
-
-        load_main_activations(0)
+        load_activations(0, 0)
         load_weights(0)
-        load_short_activations(0)
+        load_activations(0, 1)
+        load_activations(0, 2)
         for g in range(1, GROUPS):
             load_weights(g)
-        load_main_activations(1)
-        load_short_activations(1)
+        for k_pass in range(PASSES):
+            load_activations(1, k_pass)
 
         vectors = keep.tile([P, 9, SLOTS], BF16)
         V_VAR, V_GAIN, V_MEAN, V_SHIFT, V_BIAS = 0, 2, 4, 6, 8
@@ -140,7 +141,16 @@ def tile_bottleneck_transformer_pb_kernel(
 
         out_slots = [out[b].rearrange("(p c) n -> p c n", c=SLOTS) for b in range(BATCH)]
 
-        def finish_group(b, g):
+        def relu_on_vector(result):
+            nc.vector.tensor_scalar_max(out=result[:], in0=result[:], scalar1=0.0)
+
+        def relu_on_scalar(result):
+            nc.scalar.activation(out=result[:], in_=result[:], func=ACT.Relu)
+
+        def relu_on_gpsimd(result):
+            nc.gpsimd.tensor_scalar(out=result[:], in0=result[:], scalar1=0.0, scalar2=0.0, op0=ALU.max, op1=ALU.add)
+
+        def finish_group(b, g, relu):
             result = results.tile([P, GROUP, POSITIONS], F32, name="result")
             for i in range(GROUP):
                 c = g * GROUP + i
@@ -155,7 +165,7 @@ def tile_bottleneck_transformer_pb_kernel(
                 nc.vector.scalar_tensor_tensor(
                     out=result[:, i, :], in0=short[:], scalar=gain[:, 1, c : c + 1], in1=main_bn[:], op0=ALU.mult, op1=ALU.add
                 )
-            nc.vector.tensor_scalar_max(out=result[:], in0=result[:], scalar1=0.0)
+            relu(result)
             nc.sync.dma_start(out=out_slots[b][:, g * GROUP : (g + 1) * GROUP, :], in_=result[:])
 
         for k_pass in range(PASSES):
@@ -164,9 +174,9 @@ def tile_bottleneck_transformer_pb_kernel(
         for g in range(GROUPS):
             if g + 1 < GROUPS:
                 quantise_weights(g + 1)
-            finish_group(0, g)
+            finish_group(0, g, relu_on_scalar if g % 2 == 0 else relu_on_vector)
             if g >= GROUPS - PASSES:
                 quantise_activations(1, g - (GROUPS - PASSES))
 
         for g in range(GROUPS):
-            finish_group(1, g)
+            finish_group(1, g, relu_on_gpsimd)

@@ -147,9 +147,6 @@ def tile_bottleneck_transformer_pb_kernel(
         def relu_on_scalar(result):
             nc.scalar.activation(out=result[:], in_=result[:], func=ACT.Relu)
 
-        def relu_on_gpsimd(result):
-            nc.gpsimd.tensor_scalar(out=result[:], in0=result[:], scalar1=0.0, scalar2=0.0, op0=ALU.max, op1=ALU.add)
-
         def finish_group(b, g, relu):
             result = results.tile([P, GROUP, POSITIONS], F32, name="result")
             for i in range(GROUP):
@@ -179,4 +176,4 @@ def tile_bottleneck_transformer_pb_kernel(
                 quantise_activations(1, g - (GROUPS - PASSES))
 
         for g in range(GROUPS):
-            finish_group(1, g, relu_on_gpsimd)
+            finish_group(1, g, relu_on_scalar if g % 4 == 0 else relu_on_vector)

@@ -24,7 +24,6 @@ C_OUT = 2048
 SLOTS = C_OUT // P
 GROUP = 2
 GROUPS = SLOTS // GROUP
-HALF = K_PASS // 2
 UNITS_PER_BANK = 2
 BANKS_PER_GROUP = GROUP * PASSES // UNITS_PER_BANK
 EPS = 1e-5
@@ -38,35 +37,43 @@ def tile_bottleneck_transformer_pb_kernel(
     nc = tc.nc
     with ExitStack() as ctx:
         keep = ctx.enter_context(tc.tile_pool(name="keep", bufs=1))
-        stage = ctx.enter_context(tc.tile_pool(name="stage", bufs=4))
-        results = ctx.enter_context(tc.tile_pool(name="results", bufs=6))
+        act_stage = ctx.enter_context(tc.tile_pool(name="act_stage", bufs=3))
+        w_stage = ctx.enter_context(tc.tile_pool(name="w_stage", bufs=4))
+        bn_stage = ctx.enter_context(tc.tile_pool(name="bn_stage", bufs=4))
+        results = ctx.enter_context(tc.tile_pool(name="results", bufs=10))
         banks = ctx.enter_context(tc.psum_pool(name="banks", bufs=8))
+        ctx.enter_context(tc.manual_schedule())
 
         w_raw = keep.tile([P, SLOTS * C_ALL], BF16)
         w_raw_slots = w_raw[:].rearrange("p (c k) -> p c k", c=SLOTS)
+        w_words = w_raw[:].bitcast(F32)
         conv3_slots = conv3_w.rearrange("(p c) k -> p c k", c=SLOTS)
         sc_slots = sc_w.rearrange("(p c) k -> p c k", c=SLOTS)
         act_raw = [keep.tile([P, 2 * PASSES, 2, POSITIONS], BF16, name="act_raw%d" % b) for b in range(BATCH)]
+        act_codes = [keep.tile([P, PASSES, POSITIONS], U32, name="act_codes%d" % b, align_bytes=64) for b in range(BATCH)]
+        act_scales = [keep.tile([P, PASSES, POSITIONS], U8, name="act_scales%d" % b, align_bytes=64) for b in range(BATCH)]
+        w_codes = keep.tile([P, SLOTS * PASSES * P], U32, align_bytes=64)
+        w_scales = keep.tile([P, SLOTS * PASSES * P], U8, align_bytes=64)
+        out_slots = [out[b].rearrange("(p c) n -> p c n", c=SLOTS) for b in range(BATCH)]
 
         def load_weights(g):
             slots = slice(g * GROUP, (g + 1) * GROUP)
             nc.sync.dma_start(out=w_raw_slots[:, slots, 0:C_MAIN], in_=conv3_slots[:, slots, :])
             nc.sync.dma_start(out=w_raw_slots[:, slots, C_MAIN:C_ALL], in_=sc_slots[:, slots, :])
 
-        def load_activations(b, k_pass):
-            rows = h_attn[b] if k_pass == 0 else x[b, (k_pass - 1) * K_PASS : k_pass * K_PASS, :]
-            nc.sync.dma_start(
-                out=act_raw[b][:, 2 * k_pass : 2 * k_pass + 2], in_=rows.rearrange("(s p e) n -> p s e n", p=P, e=2)
-            )
+        def load_activations(b):
+            for k_pass in range(PASSES):
+                rows = h_attn[b] if k_pass == 0 else x[b, (k_pass - 1) * K_PASS : k_pass * K_PASS, :]
+                nc.sync.dma_start(
+                    out=act_raw[b][:, 2 * k_pass : 2 * k_pass + 2], in_=rows.rearrange("(s p e) n -> p s e n", p=P, e=2)
+                )
 
-        load_activations(0, 0)
-        load_weights(0)
-        load_activations(0, 1)
-        load_activations(0, 2)
-        for g in range(1, GROUPS):
+        load_activations(0)
+        for g in range(GROUPS // 2):
             load_weights(g)
-        for k_pass in range(PASSES):
-            load_activations(1, k_pass)
+        load_activations(1)
+        for g in range(GROUPS // 2, GROUPS):
+            load_weights(g)
 
         vectors = keep.tile([P, 9, SLOTS], BF16)
         V_VAR, V_GAIN, V_MEAN, V_SHIFT, V_BIAS = 0, 2, 4, 6, 8
@@ -76,55 +83,48 @@ def tile_bottleneck_transformer_pb_kernel(
         identity = keep.tile([P, P], F32)
         make_identity(nc, identity[:])
 
-        spread = keep.tile([P, 2, SLOTS], F32)
-        nc.vector.tensor_scalar_add(out=spread[:], in0=vectors[:, V_VAR : V_VAR + 2, :], scalar1=EPS)
-        nc.scalar.sqrt(out=spread[:], in_=spread[:])
-        gain = keep.tile([P, 2, SLOTS], F32)
-        nc.vector.reciprocal(out=gain[:], in_=spread[:])
-        nc.vector.tensor_mul(out=gain[:], in0=gain[:], in1=vectors[:, V_GAIN : V_GAIN + 2, :])
-        centre = keep.tile([P, 2, SLOTS], F32)
-        nc.vector.tensor_copy(out=centre[:, 0, :], in_=vectors[:, V_MEAN, :])
-        nc.vector.tensor_sub(out=centre[:, 1, :], in0=vectors[:, V_MEAN + 1, :], in1=vectors[:, V_BIAS, :])
-        nc.vector.tensor_mul(out=centre[:], in0=centre[:], in1=gain[:])
-        shift = keep.tile([P, SLOTS], F32)
-        nc.vector.tensor_add(out=shift[:], in0=vectors[:, V_SHIFT, :], in1=vectors[:, V_SHIFT + 1, :])
-        nc.vector.tensor_sub(out=shift[:], in0=shift[:], in1=centre[:, 0, :])
-        nc.vector.tensor_sub(out=shift[:], in0=shift[:], in1=centre[:, 1, :])
+        act_grouped = {}
 
-        act_codes = [keep.tile([P, PASSES, POSITIONS], U32, name="act_codes%d" % b, align_bytes=64) for b in range(BATCH)]
-        act_scales = [keep.tile([P, PASSES, POSITIONS], U8, name="act_scales%d" % b, align_bytes=64) for b in range(BATCH)]
-        w_codes = keep.tile([P, SLOTS * PASSES * P], U32, align_bytes=64)
-        w_scales = keep.tile([P, SLOTS * PASSES * P], U8, align_bytes=64)
-
-        def quantise_activations(b, k_pass):
+        def regroup_activations(b, k_pass):
             rows = act_raw[b][:, 2 * k_pass : 2 * k_pass + 2]
-            grouped = stage.tile([P, POSITIONS, PACK], BF16, name="act_grouped", align_bytes=64)
+            grouped = act_stage.tile([P, POSITIONS, PACK], BF16, name="act_grouped", align_bytes=64)
             nc.vector.tensor_copy(
                 out=grouped[:].rearrange("p (c i) t -> p c t i", i=4),
                 in_=rows.rearrange("p s e (c i) -> p c (s e) i", i=4),
             )
+            act_grouped[(b, k_pass)] = grouped
+
+        def quantise_activations(b, k_pass):
             nc.vector.quantize_mx(
                 out=act_codes[b][:, k_pass, :].bitcast(FP8X4),
                 scales=act_scales[b][:, k_pass, :],
-                in_=grouped[:].rearrange("p n t -> p (n t)"),
+                in_=act_grouped[(b, k_pass)][:].rearrange("p n t -> p (n t)"),
             )
 
-        w_words = w_raw[:].bitcast(F32)
+        turned = {}
 
-        def quantise_weights(g):
+        def transpose_weights(g):
             for j in range(g * BANKS_PER_GROUP, (g + 1) * BANKS_PER_GROUP):
-                turned = banks.tile([P, UNITS_PER_BANK, 2, P], F32, name="turned", tag="bank")
+                turned[j] = banks.tile([P, UNITS_PER_BANK, 2, P], F32, name="turned", tag="bank")
                 for a in range(UNITS_PER_BANK):
                     for u in range(2):
                         first = ((j * UNITS_PER_BANK + a) * 2 + u) * P
-                        nc.tensor.transpose(turned[:, a, u, :], w_words[:, first : first + P], identity[:])
-                grouped = stage.tile([P, UNITS_PER_BANK * P * PACK], BF16, name="w_grouped", align_bytes=64)
+                        nc.tensor.transpose(turned[j][:, a, u, :], w_words[:, first : first + P], identity[:])
+
+        w_grouped = {}
+
+        def copy_out_weights(g):
+            for j in range(g * BANKS_PER_GROUP, (g + 1) * BANKS_PER_GROUP):
+                w_grouped[j] = w_stage.tile([P, UNITS_PER_BANK * P * PACK], BF16, name="w_grouped", align_bytes=64)
                 nc.scalar.copy(
-                    out=grouped[:].bitcast(F32).rearrange("p (a m u) -> p a m u", a=UNITS_PER_BANK, u=2),
-                    in_=turned[:].rearrange("p a u m -> p a m u"),
+                    out=w_grouped[j][:].bitcast(F32).rearrange("p (a m u) -> p a m u", a=UNITS_PER_BANK, u=2),
+                    in_=turned[j][:].rearrange("p a u m -> p a m u"),
                 )
+
+        def quantise_weights(g):
+            for j in range(g * BANKS_PER_GROUP, (g + 1) * BANKS_PER_GROUP):
                 cols = slice(j * UNITS_PER_BANK * P, (j + 1) * UNITS_PER_BANK * P)
-                nc.vector.quantize_mx(out=w_codes[:, cols].bitcast(FP8X4), scales=w_scales[:, cols], in_=grouped[:])
+                nc.vector.quantize_mx(out=w_codes[:, cols].bitcast(FP8X4), scales=w_scales[:, cols], in_=w_grouped[j][:])
 
         def multiply(acc, b, c, passes):
             for k_pass in passes:
@@ -139,41 +139,79 @@ def tile_bottleneck_transformer_pb_kernel(
                     stop=(k_pass == passes[-1]),
                 )
 
-        out_slots = [out[b].rearrange("(p c) n -> p c n", c=SLOTS) for b in range(BATCH)]
-
-        def relu_on_vector(result):
-            nc.vector.tensor_scalar_max(out=result[:], in0=result[:], scalar1=0.0)
-
-        def relu_on_scalar(result):
-            nc.scalar.activation(out=result[:], in_=result[:], func=ACT.Relu)
-
-        def finish_group(b, g, relu):
-            result = results.tile([P, GROUP, POSITIONS], F32, name="result")
-            for i in range(GROUP):
-                c = g * GROUP + i
+        def multiply_group(b, g):
+            products = []
+            for c in range(g * GROUP, (g + 1) * GROUP):
                 main = banks.tile([P, POSITIONS], F32, name="main", tag="bank")
                 multiply(main, b, c, (0,))
                 short = banks.tile([P, POSITIONS], F32, name="short", tag="bank")
                 multiply(short, b, c, (1, 2))
-                main_bn = stage.tile([P, POSITIONS], F32, name="main_bn")
+                products.append((c, main, short))
+            return products
+
+        def batch_norms_and_sum(products):
+            result = results.tile([P, GROUP, POSITIONS], F32, name="result")
+            main_bn = []
+            for c, main, short in products:
+                main_bn.append(bn_stage.tile([P, POSITIONS], F32, name="main_bn"))
                 nc.scalar.activation(
-                    out=main_bn[:], in_=main[:], func=ACT.Identity, scale=gain[:, 0, c : c + 1], bias=shift[:, c : c + 1]
+                    out=main_bn[-1][:], in_=main[:], func=ACT.Identity, scale=gain[:, 0, c : c + 1], bias=shift[:, c : c + 1]
                 )
+            for i, (c, main, short) in enumerate(products):
                 nc.vector.scalar_tensor_tensor(
-                    out=result[:, i, :], in0=short[:], scalar=gain[:, 1, c : c + 1], in1=main_bn[:], op0=ALU.mult, op1=ALU.add
+                    out=result[:, i, :], in0=short[:], scalar=gain[:, 1, c : c + 1], in1=main_bn[i][:], op0=ALU.mult, op1=ALU.add
                 )
-            relu(result)
+            return result
+
+        def relu_and_store(b, g, result):
+            if g % 4 == 1:
+                nc.scalar.activation(out=result[:], in_=result[:], func=ACT.Relu)
+            else:
+                nc.vector.tensor_scalar_max(out=result[:], in0=result[:], scalar1=0.0)
             nc.sync.dma_start(out=out_slots[b][:, g * GROUP : (g + 1) * GROUP, :], in_=result[:])
 
-        for k_pass in range(PASSES):
-            quantise_activations(0, k_pass)
+        spread = keep.tile([P, 2, SLOTS], F32)
+        gain = keep.tile([P, 2, SLOTS], F32)
+        centre = keep.tile([P, 2, SLOTS], F32)
+        shift = keep.tile([P, SLOTS], F32)
+        nc.vector.tensor_scalar_add(out=spread[:], in0=vectors[:, V_VAR : V_VAR + 2, :], scalar1=EPS)
+        nc.scalar.sqrt(out=spread[:], in_=spread[:])
+        regroup_activations(0, 0)
+        regroup_activations(0, 1)
+        quantise_activations(0, 0)
+        regroup_activations(0, 2)
+        quantise_activations(0, 1)
+        nc.vector.reciprocal(out=gain[:], in_=spread[:])
+        nc.vector.tensor_mul(out=gain[:], in0=gain[:], in1=vectors[:, V_GAIN : V_GAIN + 2, :])
+        nc.vector.tensor_copy(out=centre[:, 0, :], in_=vectors[:, V_MEAN, :])
+        nc.vector.tensor_sub(out=centre[:, 1, :], in0=vectors[:, V_MEAN + 1, :], in1=vectors[:, V_BIAS, :])
+        nc.vector.tensor_mul(out=centre[:], in0=centre[:], in1=gain[:])
+        nc.vector.tensor_add(out=shift[:], in0=vectors[:, V_SHIFT, :], in1=vectors[:, V_SHIFT + 1, :])
+        nc.vector.tensor_sub(out=shift[:], in0=shift[:], in1=centre[:, 0, :])
+        nc.vector.tensor_sub(out=shift[:], in0=shift[:], in1=centre[:, 1, :])
+        quantise_activations(0, 2)
+        transpose_weights(0)
+        copy_out_weights(0)
+        transpose_weights(1)
         quantise_weights(0)
+
+        waiting = []
         for g in range(GROUPS):
             if g + 1 < GROUPS:
+                copy_out_weights(g + 1)
                 quantise_weights(g + 1)
-            finish_group(0, g, relu_on_scalar if g % 2 == 0 else relu_on_vector)
-            if g >= GROUPS - PASSES:
-                quantise_activations(1, g - (GROUPS - PASSES))
+            products = multiply_group(0, g)
+            if g + 2 < GROUPS:
+                transpose_weights(g + 2)
+            waiting.append((0, g, batch_norms_and_sum(products)))
+            if len(waiting) > 1:
+                relu_and_store(*waiting.pop(0))
+            if 1 <= g <= PASSES:
+                regroup_activations(1, g - 1)
+            if 2 <= g <= PASSES + 1:
+                quantise_activations(1, g - 2)
 
         for g in range(GROUPS):
-            finish_group(1, g, relu_on_scalar if g % 4 == 0 else relu_on_vector)
+            waiting.append((1, g, batch_norms_and_sum(multiply_group(1, g))))
+            relu_and_store(*waiting.pop(0))
+        relu_and_store(*waiting.pop(0))

from contextlib import ExitStack

import concourse.mybir as mybir
from concourse.masks import make_identity

F32 = mybir.dt.float32
BF16 = mybir.dt.bfloat16
U32 = mybir.dt.uint32
U8 = mybir.dt.uint8
FP8X4 = mybir.dt.float8_e4m3fn_x4
ACT = mybir.ActivationFunctionType
ALU = mybir.AluOpType

P = 128
PACK = 4
K_PASS = P * PACK
BATCH = 2
POSITIONS = 512
C_MAIN = 512
C_SHORT = 1024
C_ALL = C_MAIN + C_SHORT
PASSES = C_ALL // K_PASS
C_OUT = 2048
SLOTS = C_OUT // P
GROUP = 2
GROUPS = SLOTS // GROUP
UNITS_PER_BANK = 2
BANKS_PER_GROUP = GROUP * PASSES // UNITS_PER_BANK
EPS = 1e-5

FLOPS = 2 * BATCH * C_OUT * C_ALL * POSITIONS


def tile_bottleneck_transformer_pb_kernel(
    tc, h_attn, x, conv3_w, bn3_g, bn3_b, bn3_m, bn3_v, sc_w, sc_b, scbn_g, scbn_b, scbn_m, scbn_v, out
):
    nc = tc.nc
    with ExitStack() as ctx:
        keep = ctx.enter_context(tc.tile_pool(name="keep", bufs=1))
        act_stage = ctx.enter_context(tc.tile_pool(name="act_stage", bufs=3))
        w_stage = ctx.enter_context(tc.tile_pool(name="w_stage", bufs=4))
        bn_stage = ctx.enter_context(tc.tile_pool(name="bn_stage", bufs=4))
        results = ctx.enter_context(tc.tile_pool(name="results", bufs=10))
        banks = ctx.enter_context(tc.psum_pool(name="banks", bufs=8))
        ctx.enter_context(tc.manual_schedule())

        w_raw = keep.tile([P, SLOTS * C_ALL], BF16)
        w_raw_slots = w_raw[:].rearrange("p (c k) -> p c k", c=SLOTS)
        w_words = w_raw[:].bitcast(F32)
        conv3_slots = conv3_w.rearrange("(p c) k -> p c k", c=SLOTS)
        sc_slots = sc_w.rearrange("(p c) k -> p c k", c=SLOTS)
        act_raw = [keep.tile([P, 2 * PASSES, 2, POSITIONS], BF16, name="act_raw%d" % b) for b in range(BATCH)]
        act_codes = [keep.tile([P, PASSES, POSITIONS], U32, name="act_codes%d" % b, align_bytes=64) for b in range(BATCH)]
        act_scales = [keep.tile([P, PASSES, POSITIONS], U8, name="act_scales%d" % b, align_bytes=64) for b in range(BATCH)]
        w_codes = keep.tile([P, SLOTS * PASSES * P], U32, align_bytes=64)
        w_scales = keep.tile([P, SLOTS * PASSES * P], U8, align_bytes=64)
        out_slots = [out[b].rearrange("(p c) n -> p c n", c=SLOTS) for b in range(BATCH)]

        def load_weights(g):
            slots = slice(g * GROUP, (g + 1) * GROUP)
            nc.sync.dma_start(out=w_raw_slots[:, slots, 0:C_MAIN], in_=conv3_slots[:, slots, :])
            nc.sync.dma_start(out=w_raw_slots[:, slots, C_MAIN:C_ALL], in_=sc_slots[:, slots, :])

        def load_activations(b):
            for k_pass in range(PASSES):
                rows = h_attn[b] if k_pass == 0 else x[b, (k_pass - 1) * K_PASS : k_pass * K_PASS, :]
                nc.sync.dma_start(
                    out=act_raw[b][:, 2 * k_pass : 2 * k_pass + 2], in_=rows.rearrange("(s p e) n -> p s e n", p=P, e=2)
                )

        load_activations(0)
        for g in range(GROUPS // 2):
            load_weights(g)
        load_activations(1)
        for g in range(GROUPS // 2, GROUPS):
            load_weights(g)

        vectors = keep.tile([P, 9, SLOTS], BF16)
        V_VAR, V_GAIN, V_MEAN, V_SHIFT, V_BIAS = 0, 2, 4, 6, 8
        for i, vec in enumerate((bn3_v, scbn_v, bn3_g, scbn_g, bn3_m, scbn_m, bn3_b, scbn_b, sc_b)):
            nc.scalar.dma_start(out=vectors[:, i, :], in_=vec.rearrange("(p c) -> p c", c=SLOTS))

        identity = keep.tile([P, P], F32)
        make_identity(nc, identity[:])

        act_grouped = {}

        def regroup_activations(b, k_pass):
            rows = act_raw[b][:, 2 * k_pass : 2 * k_pass + 2]
            grouped = act_stage.tile([P, POSITIONS, PACK], BF16, name="act_grouped", align_bytes=64)
            nc.vector.tensor_copy(
                out=grouped[:].rearrange("p (c i) t -> p c t i", i=4),
                in_=rows.rearrange("p s e (c i) -> p c (s e) i", i=4),
            )
            act_grouped[(b, k_pass)] = grouped

        def quantise_activations(b, k_pass):
            nc.vector.quantize_mx(
                out=act_codes[b][:, k_pass, :].bitcast(FP8X4),
                scales=act_scales[b][:, k_pass, :],
                in_=act_grouped[(b, k_pass)][:].rearrange("p n t -> p (n t)"),
            )

        turned = {}

        def transpose_weights(g):
            for j in range(g * BANKS_PER_GROUP, (g + 1) * BANKS_PER_GROUP):
                turned[j] = banks.tile([P, UNITS_PER_BANK, 2, P], F32, name="turned", tag="bank")
                for a in range(UNITS_PER_BANK):
                    for u in range(2):
                        first = ((j * UNITS_PER_BANK + a) * 2 + u) * P
                        nc.tensor.transpose(turned[j][:, a, u, :], w_words[:, first : first + P], identity[:])

        w_grouped = {}

        def copy_out_weights(g):
            for j in range(g * BANKS_PER_GROUP, (g + 1) * BANKS_PER_GROUP):
                w_grouped[j] = w_stage.tile([P, UNITS_PER_BANK * P * PACK], BF16, name="w_grouped", align_bytes=64)
                nc.scalar.copy(
                    out=w_grouped[j][:].bitcast(F32).rearrange("p (a m u) -> p a m u", a=UNITS_PER_BANK, u=2),
                    in_=turned[j][:].rearrange("p a u m -> p a m u"),
                )

        def quantise_weights(g):
            for j in range(g * BANKS_PER_GROUP, (g + 1) * BANKS_PER_GROUP):
                cols = slice(j * UNITS_PER_BANK * P, (j + 1) * UNITS_PER_BANK * P)
                nc.vector.quantize_mx(out=w_codes[:, cols].bitcast(FP8X4), scales=w_scales[:, cols], in_=w_grouped[j][:])

        def multiply(acc, b, c, passes):
            for k_pass in passes:
                cols = slice((c * PASSES + k_pass) * P, (c * PASSES + k_pass + 1) * P)
                nc.tensor.matmul_mx(
                    out=acc[:],
                    lhsT=w_codes[:, cols].bitcast(FP8X4),
                    lhsT_scale=w_scales[:, cols],
                    rhs=act_codes[b][:, k_pass, :].bitcast(FP8X4),
                    rhs_scale=act_scales[b][:, k_pass, :],
                    start=(k_pass == passes[0]),
                    stop=(k_pass == passes[-1]),
                )

        def multiply_group(b, g):
            products = []
            for c in range(g * GROUP, (g + 1) * GROUP):
                main = banks.tile([P, POSITIONS], F32, name="main", tag="bank")
                multiply(main, b, c, (0,))
                short = banks.tile([P, POSITIONS], F32, name="short", tag="bank")
                multiply(short, b, c, (1, 2))
                products.append((c, main, short))
            return products

        def batch_norms_and_sum(products):
            result = results.tile([P, GROUP, POSITIONS], F32, name="result")
            main_bn = []
            for c, main, short in products:
                main_bn.append(bn_stage.tile([P, POSITIONS], F32, name="main_bn"))
                nc.scalar.activation(
                    out=main_bn[-1][:], in_=main[:], func=ACT.Identity, scale=gain[:, 0, c : c + 1], bias=shift[:, c : c + 1]
                )
            for i, (c, main, short) in enumerate(products):
                nc.vector.scalar_tensor_tensor(
                    out=result[:, i, :], in0=short[:], scalar=gain[:, 1, c : c + 1], in1=main_bn[i][:], op0=ALU.mult, op1=ALU.add
                )
            return result

        def relu_and_store(b, g, result):
            if g % 4 == 1:
                nc.scalar.activation(out=result[:], in_=result[:], func=ACT.Relu)
            else:
                nc.vector.tensor_scalar_max(out=result[:], in0=result[:], scalar1=0.0)
            nc.sync.dma_start(out=out_slots[b][:, g * GROUP : (g + 1) * GROUP, :], in_=result[:])

        spread = keep.tile([P, 2, SLOTS], F32)
        gain = keep.tile([P, 2, SLOTS], F32)
        centre = keep.tile([P, 2, SLOTS], F32)
        shift = keep.tile([P, SLOTS], F32)
        nc.vector.tensor_scalar_add(out=spread[:], in0=vectors[:, V_VAR : V_VAR + 2, :], scalar1=EPS)
        nc.scalar.sqrt(out=spread[:], in_=spread[:])
        regroup_activations(0, 0)
        regroup_activations(0, 1)
        quantise_activations(0, 0)
        regroup_activations(0, 2)
        quantise_activations(0, 1)
        nc.vector.reciprocal(out=gain[:], in_=spread[:])
        nc.vector.tensor_mul(out=gain[:], in0=gain[:], in1=vectors[:, V_GAIN : V_GAIN + 2, :])
        nc.vector.tensor_copy(out=centre[:, 0, :], in_=vectors[:, V_MEAN, :])
        nc.vector.tensor_sub(out=centre[:, 1, :], in0=vectors[:, V_MEAN + 1, :], in1=vectors[:, V_BIAS, :])
        nc.vector.tensor_mul(out=centre[:], in0=centre[:], in1=gain[:])
        nc.vector.tensor_add(out=shift[:], in0=vectors[:, V_SHIFT, :], in1=vectors[:, V_SHIFT + 1, :])
        nc.vector.tensor_sub(out=shift[:], in0=shift[:], in1=centre[:, 0, :])
        nc.vector.tensor_sub(out=shift[:], in0=shift[:], in1=centre[:, 1, :])
        quantise_activations(0, 2)
        transpose_weights(0)
        copy_out_weights(0)
        transpose_weights(1)
        quantise_weights(0)

        waiting = []
        for g in range(GROUPS):
            if g + 1 < GROUPS:
                copy_out_weights(g + 1)
                quantise_weights(g + 1)
            products = multiply_group(0, g)
            if g + 2 < GROUPS:
                transpose_weights(g + 2)
            waiting.append((0, g, batch_norms_and_sum(products)))
            if len(waiting) > 1:
                relu_and_store(*waiting.pop(0))
            if 1 <= g <= PASSES:
                regroup_activations(1, g - 1)
            if 2 <= g <= PASSES + 1:
                quantise_activations(1, g - 2)

        for g in range(GROUPS):
            waiting.append((1, g, batch_norms_and_sum(multiply_group(1, g))))
            relu_and_store(*waiting.pop(0))
        relu_and_store(*waiting.pop(0))
